import numpy as np
import ml_dtypes


def mxq(x, axis, fmt="e4m3"):
    dtype, down = {"e4m3": (ml_dtypes.float8_e4m3fn, 7), "e5m2": (ml_dtypes.float8_e5m2, 14)}[fmt]
    v = np.moveaxis(np.asarray(x, np.float32).astype(ml_dtypes.bfloat16).astype(np.float64), axis, -1)
    blocks = v.reshape(v.shape[:-1] + (-1, 32))
    amax = np.abs(blocks).max(-1, keepdims=True)
    byte = np.maximum(np.where(amax > 0, np.frexp(amax)[1] - 1 + 127, 0) - down, 1)
    scale = np.exp2(byte - 127.0)
    codes = (blocks / scale).astype(np.float32).astype(dtype).astype(np.float64)
    return np.moveaxis((codes * scale).reshape(v.shape), -1, axis)


WIDE = False


def mx_kscale(k):
    if not WIDE:
        return np.ones(k)
    levels = np.array([10, -10, 5, -5, 0])
    a = np.random.permutation(np.resize(levels, k // 512 * 4)).reshape(k // 512, 4)
    idx = np.arange(k)
    return np.exp2(a[idx // 512, idx % 128 // 32])


BF16 = ml_dtypes.bfloat16


def bf(x):
    return np.asarray(x, np.float32).astype(BF16)


def f64(x):
    return np.asarray(x).astype(np.float64)


B, S, HID, NH, NOPE, ROPE, VD, KV_RANK, SW, QB = 1, 8192, 512, 2, 64, 64, 128, 512, 384, 128
QK = NOPE + ROPE


def rotate_half(x):
    h = x.shape[-1] // 2
    return np.concatenate([-x[..., h:], x[..., :h]], axis=-1)


def rope_tables():
    pos = np.arange(S, dtype=np.float64)
    inv = 1.0 / (10000.0 ** (np.arange(0, ROPE, 2, dtype=np.float64) / ROPE))
    ang = pos[:, None] * inv[None, :]
    ang = np.concatenate([ang, ang], axis=-1)
    return bf(np.broadcast_to(np.cos(ang)[None], (B, S, ROPE))), bf(np.broadcast_to(np.sin(ang)[None], (B, S, ROPE)))


def setup_inputs():
    s = mx_kscale(HID)
    cos, sin = rope_tables()
    return {"hidden_states": bf(np.random.standard_normal((B, S, HID)) * s), "cos": cos, "sin": sin,
            "Wq": bf(np.random.standard_normal((HID, NH * QK)) * 2.0 / np.sqrt(HID) / s[:, None]),
            "bq": bf(np.random.standard_normal(NH * QK) * 0.2)}


def reference(hidden_states, cos, sin, Wq, bq):
    q = ((mxq(f64(hidden_states), 2, "e4m3") @ mxq(f64(Wq), 0, "e4m3")) + f64(bq)).reshape(B, S, NH, QK).transpose(0, 2, 1, 3)
    q_nope, q_rope = q[..., :NOPE], q[..., NOPE:]
    c, si = f64(cos)[:, None], f64(sin)[:, None]
    q_rope = q_rope * c + rotate_half(q_rope) * si
    return np.concatenate([q_nope, q_rope], axis=-1)

@@ -1,0 +1,185 @@
+import concourse.mybir as mybir
+from concourse.masks import make_identity
+
+F32 = mybir.dt.float32
+BF16 = mybir.dt.bfloat16
+U32 = mybir.dt.uint32
+U8 = mybir.dt.uint8
+FP8X4 = mybir.dt.float8_e4m3fn_x4
+ADD = mybir.AluOpType.add
+SUBTRACT = mybir.AluOpType.subtract
+MULT = mybir.AluOpType.mult
+
+P = 128
+TOKENS = 8192
+HID = 512
+HEADS = 2
+HEAD_DIM = 128
+NOPE = 64
+ROPE = 64
+HALF = ROPE // 2
+FEATURES = HEADS * HEAD_DIM
+PACK = 4
+SLOTS = TOKENS // P
+GROUP = 4
+CHUNK = 8
+TABLE_SLOTS = 32
+
+FLOPS = 2 * TOKENS * HID * FEATURES
+
+
+def tile_gptossmlaattention_pb_t_kernel(tc, hidden_states, cos, sin, Wq, bq, out):
+    nc = tc.nc
+    hidden_view = hidden_states.flatten_outer_dims().rearrange("(p t) k -> p t k", t=SLOTS)
+    cos_view = cos.flatten_outer_dims().rearrange("(p t) c -> p t c", t=SLOTS)
+    sin_view = sin.flatten_outer_dims().rearrange("(p t) c -> p t c", t=SLOTS)
+    out_view = out.flatten_outer_dims().rearrange("(h p t) d -> p h t d", h=HEADS, t=SLOTS)
+
+    with tc.tile_pool(name="const", bufs=1) as const, tc.tile_pool(
+        name="resident", bufs=SLOTS // CHUNK
+    ) as resident, tc.tile_pool(name="tables", bufs=SLOTS // TABLE_SLOTS) as tables, tc.tile_pool(
+        name="stage", bufs=3
+    ) as stage, tc.psum_pool(name="psum_t", bufs=3) as psum_t, tc.psum_pool(
+        name="psum_q", bufs=4
+    ) as psum_q, tc.psum_pool(name="psum_b", bufs=1) as psum_b:
+        w_raw = const.tile([P, PACK, FEATURES], BF16)
+        for u in range(2):
+            nc.sync.dma_start(
+                out=w_raw[:, 2 * u : 2 * u + 2, :],
+                in_=Wq[256 * u : 256 * u + 256, :].rearrange("(p e) c -> p e c", e=2),
+            )
+        x_chunks = []
+        cos_parts = []
+        sin_parts = []
+        for c in range(SLOTS // CHUNK):
+            x_sb = resident.tile([P, CHUNK, HID], BF16)
+            nc.sync.dma_start(out=x_sb[:], in_=hidden_view[:, c * CHUNK : (c + 1) * CHUNK, :])
+            x_chunks.append(x_sb)
+            if c % (TABLE_SLOTS // CHUNK) == 0:
+                part = slice(c * CHUNK, c * CHUNK + TABLE_SLOTS)
+                cos_sb = tables.tile([P, TABLE_SLOTS, ROPE], BF16)
+                nc.sync.dma_start(out=cos_sb[:], in_=cos_view[:, part, :])
+                cos_parts.append(cos_sb)
+                sin_sb = tables.tile([P, TABLE_SLOTS, ROPE], BF16)
+                nc.sync.dma_start(out=sin_sb[:], in_=sin_view[:, part, :])
+                sin_parts.append(sin_sb)
+
+        ident = const.tile([P, P], F32)
+        make_identity(nc, ident[:])
+
+        bias_row = const.tile([P, FEATURES], BF16)
+        nc.vector.memset(bias_row[:], 0.0)
+        nc.scalar.dma_start(out=bias_row[0:1, :], in_=bq.rearrange("(o f) -> o f", o=1))
+        ones = const.tile([P, P], BF16)
+        nc.vector.memset(ones[:], 1.0)
+        bias_ps = psum_b.tile([P, FEATURES], F32)
+        nc.tensor.matmul(out=bias_ps[:], lhsT=ones[:], rhs=bias_row[:], start=True, stop=True)
+        bias_sb = const.tile([P, FEATURES], F32)
+        nc.vector.tensor_copy(out=bias_sb[:], in_=bias_ps[:])
+
+        w_grouped = const.tile([P, FEATURES, PACK], BF16, align_bytes=64)
+        nc.vector.tensor_copy(out=w_grouped[:], in_=w_raw[:].rearrange("p t c -> p c t"))
+        w_codes = const.tile([P, FEATURES], U32, align_bytes=64)
+        w_scales = const.tile([P, FEATURES], U8, align_bytes=64)
+        nc.vector.quantize_mx(
+            out=w_codes[:].bitcast(FP8X4),
+            scales=w_scales[:],
+            in_=w_grouped[:].rearrange("p c t -> p (c t)"),
+        )
+
+        bias_pair = (
+            bias_sb[:]
+            .rearrange("p (h d) -> p h d", h=HEADS)
+            .unsqueeze(1)
+            .to_broadcast([P, 2, HEADS, HEAD_DIM])
+        )
+
+        for c in range(SLOTS // CHUNK):
+            x_words = x_chunks[c][:].bitcast(F32)
+            out_sb = resident.tile([P, HEADS, CHUNK, HEAD_DIM], F32)
+            out_slots = out_sb[:].rearrange("p h t d -> p t h d")
+            for g in range(CHUNK // GROUP):
+                first = g * GROUP
+                grouped = stage.tile([P, GROUP * P * PACK], BF16, align_bytes=64)
+                grouped_words = grouped[:].bitcast(F32).rearrange("p (r u) -> p r u", u=2)
+                for pair in range(GROUP // 2):
+                    x_t = psum_t.tile([P, 2, 2 * P], F32)
+                    for i in range(2):
+                        for u in range(2):
+                            nc.tensor.transpose(
+                                x_t[:, u, i * P : (i + 1) * P],
+                                x_words[:, first + 2 * pair + i, u * P : (u + 1) * P],
+                                ident[:],
+                            )
+                    nc.scalar.copy(
+                        out=grouped_words[:, pair * 2 * P : (pair + 1) * 2 * P, :],
+                        in_=x_t[:].rearrange("p u r -> p r u"),
+                    )
+                codes = stage.tile([P, GROUP * P], U32, align_bytes=64)
+                scales = stage.tile([P, GROUP * P], U8, align_bytes=64)
+                nc.vector.quantize_mx(
+                    out=codes[:].bitcast(FP8X4), scales=scales[:], in_=grouped[:]
+                )
+
+                x_rope = stage.tile([P, GROUP, HEADS, ROPE], F32)
+                for pair in range(GROUP // 2):
+                    q_ps = psum_q.tile([P, 2, FEATURES], F32)
+                    for i in range(2):
+                        cols = slice((2 * pair + i) * P, (2 * pair + i + 1) * P)
+                        nc.tensor.matmul_mx(
+                            out=q_ps[:, i, :],
+                            lhsT=codes[:, cols].bitcast(FP8X4),
+                            lhsT_scale=scales[:, cols],
+                            rhs=w_codes[:].bitcast(FP8X4),
+                            rhs_scale=w_scales[:],
+                            start=True,
+                            stop=True,
+                        )
+                    q_heads = q_ps[:].rearrange("p i (h d) -> p i h d", h=HEADS)
+                    slots = slice(first + 2 * pair, first + 2 * pair + 2)
+                    nc.vector.tensor_tensor(
+                        out=out_slots[:, slots, :, 0:NOPE],
+                        in0=q_heads[:, :, :, 0:NOPE],
+                        in1=bias_pair[:, :, :, 0:NOPE],
+                        op=ADD,
+                    )
+                    nc.vector.tensor_tensor(
+                        out=x_rope[:, 2 * pair : 2 * pair + 2, :, :],
+                        in0=q_heads[:, :, :, NOPE:HEAD_DIM],
+                        in1=bias_pair[:, :, :, NOPE:HEAD_DIM],
+                        op=ADD,
+                    )
+
+                slot0 = c * CHUNK + first
+                in_part = slice(slot0 % TABLE_SLOTS, slot0 % TABLE_SLOTS + GROUP)
+                both_heads = [P, GROUP, HEADS, ROPE]
+                cos_g = cos_parts[slot0 // TABLE_SLOTS][:, in_part, :].unsqueeze(2).to_broadcast(both_heads)
+                sin_g = sin_parts[slot0 // TABLE_SLOTS][:, in_part, :].unsqueeze(2).to_broadcast(both_heads)
+                out_rope = out_slots[:, first : first + GROUP, :, NOPE:HEAD_DIM]
+                turned = stage.tile([P, GROUP, HEADS, ROPE], F32)
+                nc.vector.tensor_tensor(out=out_rope, in0=x_rope[:], in1=cos_g, op=MULT)
+                nc.vector.tensor_tensor(
+                    out=turned[:, :, :, 0:HALF],
+                    in0=x_rope[:, :, :, HALF:ROPE],
+                    in1=sin_g[:, :, :, 0:HALF],
+                    op=MULT,
+                )
+                nc.vector.tensor_tensor(
+                    out=turned[:, :, :, HALF:ROPE],
+                    in0=x_rope[:, :, :, 0:HALF],
+                    in1=sin_g[:, :, :, HALF:ROPE],
+                    op=MULT,
+                )
+                nc.vector.tensor_tensor(
+                    out=out_rope[:, :, :, 0:HALF],
+                    in0=out_rope[:, :, :, 0:HALF],
+                    in1=turned[:, :, :, 0:HALF],
+                    op=SUBTRACT,
+                )
+                nc.vector.tensor_tensor(
+                    out=out_rope[:, :, :, HALF:ROPE],
+                    in0=out_rope[:, :, :, HALF:ROPE],
+                    in1=turned[:, :, :, HALF:ROPE],
+                    op=ADD,
+                )
+            nc.sync.dma_start(out=out_view[:, :, c * CHUNK : (c + 1) * CHUNK, :], in_=out_sb[:])

@@ -9,6 +9,7 @@ FP8X4 = mybir.dt.float8_e4m3fn_x4
 ADD = mybir.AluOpType.add
 SUBTRACT = mybir.AluOpType.subtract
 MULT = mybir.AluOpType.mult
+IDENTITY = mybir.ActivationFunctionType.Identity
 
 P = 128
 TOKENS = 8192
@@ -22,7 +23,9 @@ FEATURES = HEADS * HEAD_DIM
 PACK = 4
 SLOTS = TOKENS // P
 GROUP = 4
+GROUPS = SLOTS // GROUP
 CHUNK = 8
+CHUNK_GROUPS = CHUNK // GROUP
 TABLE_SLOTS = 32
 
 FLOPS = 2 * TOKENS * HID * FEATURES
@@ -39,9 +42,11 @@ def tile_gptossmlaattention_pb_t_kernel(tc, hidden_states, cos, sin, Wq, bq, out
         name="resident", bufs=SLOTS // CHUNK
     ) as resident, tc.tile_pool(name="tables", bufs=SLOTS // TABLE_SLOTS) as tables, tc.tile_pool(
         name="stage", bufs=3
-    ) as stage, tc.psum_pool(name="psum_t", bufs=3) as psum_t, tc.psum_pool(
-        name="psum_q", bufs=4
-    ) as psum_q, tc.psum_pool(name="psum_b", bufs=1) as psum_b:
+    ) as stage, tc.psum_pool(name="psum_setup", bufs=1) as psum_setup, tc.psum_pool(
+        name="psum_t", bufs=2
+    ) as psum_t, tc.psum_pool(name="psum_nope", bufs=2) as psum_nope, tc.psum_pool(
+        name="psum_rope_t", bufs=1
+    ) as psum_rope_t, tc.psum_pool(name="psum_rope", bufs=2) as psum_rope, tc.manual_schedule():
         w_raw = const.tile([P, PACK, FEATURES], BF16)
         for u in range(2):
             nc.sync.dma_start(
@@ -67,119 +72,193 @@ def tile_gptossmlaattention_pb_t_kernel(tc, hidden_states, cos, sin, Wq, bq, out
         ident = const.tile([P, P], F32)
         make_identity(nc, ident[:])
 
+        w_grouped = const.tile([P, 2, P, PACK], BF16, align_bytes=64)
+        w_by_kind = w_raw[:].rearrange("p t (h x d) -> p x h d t", h=HEADS, x=2)
+        bq_by_kind = bq.rearrange("(o h x d) -> o x h d", o=1, h=HEADS, x=2)
         bias_row = const.tile([P, FEATURES], BF16)
         nc.vector.memset(bias_row[:], 0.0)
-        nc.scalar.dma_start(out=bias_row[0:1, :], in_=bq.rearrange("(o f) -> o f", o=1))
         ones = const.tile([P, P], BF16)
         nc.vector.memset(ones[:], 1.0)
-        bias_ps = psum_b.tile([P, FEATURES], F32)
-        nc.tensor.matmul(out=bias_ps[:], lhsT=ones[:], rhs=bias_row[:], start=True, stop=True)
-        bias_sb = const.tile([P, FEATURES], F32)
-        nc.vector.tensor_copy(out=bias_sb[:], in_=bias_ps[:])
-
-        w_grouped = const.tile([P, FEATURES, PACK], BF16, align_bytes=64)
-        nc.vector.tensor_copy(out=w_grouped[:], in_=w_raw[:].rearrange("p t c -> p c t"))
+        for x in range(2):
+            nc.scalar.dma_start(
+                out=bias_row[0:1, x * P : (x + 1) * P].rearrange("o (h d) -> o h d", h=HEADS),
+                in_=bq_by_kind[:, x],
+            )
+            nc.vector.tensor_copy(
+                out=w_grouped[:, x].rearrange("p (h d) t -> p h d t", h=HEADS), in_=w_by_kind[:, x]
+            )
         w_codes = const.tile([P, FEATURES], U32, align_bytes=64)
         w_scales = const.tile([P, FEATURES], U8, align_bytes=64)
         nc.vector.quantize_mx(
             out=w_codes[:].bitcast(FP8X4),
             scales=w_scales[:],
-            in_=w_grouped[:].rearrange("p c t -> p (c t)"),
+            in_=w_grouped[:].rearrange("p x c t -> p (x c t)"),
         )
+        stay = slice(0, P)
+        turn = slice(P, 2 * P)
 
-        bias_pair = (
-            bias_sb[:]
-            .rearrange("p (h d) -> p h d", h=HEADS)
-            .unsqueeze(1)
-            .to_broadcast([P, 2, HEADS, HEAD_DIM])
+        setup_ps = psum_setup.tile([P, FEATURES + ROPE], F32)
+        nc.tensor.matmul(
+            out=setup_ps[:, 0:FEATURES], lhsT=ones[:], rhs=bias_row[:], start=True, stop=True
         )
+        nc.tensor.matmul(
+            out=setup_ps[:, FEATURES : FEATURES + ROPE],
+            lhsT=bias_row[:, turn],
+            rhs=ones[:, 0:ROPE],
+            start=True,
+            stop=True,
+        )
+        bias_stay = const.tile([P, HEADS, NOPE], F32)
+        nc.vector.tensor_copy(
+            out=bias_stay[:], in_=setup_ps[:, stay].rearrange("p (h d) -> p h d", h=HEADS)
+        )
+        bias_turn = const.tile([P, 1], F32)
+        nc.vector.tensor_copy(out=bias_turn[:], in_=setup_ps[:, FEATURES : FEATURES + 1])
 
-        for c in range(SLOTS // CHUNK):
-            x_words = x_chunks[c][:].bitcast(F32)
-            out_sb = resident.tile([P, HEADS, CHUNK, HEAD_DIM], F32)
-            out_slots = out_sb[:].rearrange("p h t d -> p t h d")
-            for g in range(CHUNK // GROUP):
-                first = g * GROUP
-                grouped = stage.tile([P, GROUP * P * PACK], BF16, align_bytes=64)
-                grouped_words = grouped[:].bitcast(F32).rearrange("p (r u) -> p r u", u=2)
-                for pair in range(GROUP // 2):
-                    x_t = psum_t.tile([P, 2, 2 * P], F32)
-                    for i in range(2):
-                        for u in range(2):
-                            nc.tensor.transpose(
-                                x_t[:, u, i * P : (i + 1) * P],
-                                x_words[:, first + 2 * pair + i, u * P : (u + 1) * P],
-                                ident[:],
-                            )
-                    nc.scalar.copy(
-                        out=grouped_words[:, pair * 2 * P : (pair + 1) * 2 * P, :],
-                        in_=x_t[:].rearrange("p u r -> p r u"),
-                    )
-                codes = stage.tile([P, GROUP * P], U32, align_bytes=64)
-                scales = stage.tile([P, GROUP * P], U8, align_bytes=64)
-                nc.vector.quantize_mx(
-                    out=codes[:].bitcast(FP8X4), scales=scales[:], in_=grouped[:]
-                )
+        grouped_of = {}
+        codes_of = {}
+        scales_of = {}
+        q_stay_of = {}
+        q_turn_t_of = {}
+        x_turn_t_of = {}
+        x_turn_of = {}
+        out_of = {}
 
-                x_rope = stage.tile([P, GROUP, HEADS, ROPE], F32)
-                for pair in range(GROUP // 2):
-                    q_ps = psum_q.tile([P, 2, FEATURES], F32)
-                    for i in range(2):
-                        cols = slice((2 * pair + i) * P, (2 * pair + i + 1) * P)
-                        nc.tensor.matmul_mx(
-                            out=q_ps[:, i, :],
-                            lhsT=codes[:, cols].bitcast(FP8X4),
-                            lhsT_scale=scales[:, cols],
-                            rhs=w_codes[:].bitcast(FP8X4),
-                            rhs_scale=w_scales[:],
-                            start=True,
-                            stop=True,
+        def transpose_hidden(g):
+            x_words = x_chunks[g // CHUNK_GROUPS][:].bitcast(F32)
+            first = (g % CHUNK_GROUPS) * GROUP
+            grouped = stage.tile([P, GROUP * P * PACK], BF16, align_bytes=64)
+            grouped_words = grouped[:].bitcast(F32).rearrange("p (r u) -> p r u", u=2)
+            for pair in range(GROUP // 2):
+                x_t = psum_t.tile([P, 2, 2 * P], F32)
+                for i in range(2):
+                    for u in range(2):
+                        nc.tensor.transpose(
+                            x_t[:, u, i * P : (i + 1) * P],
+                            x_words[:, first + 2 * pair + i, u * P : (u + 1) * P],
+                            ident[:],
                         )
-                    q_heads = q_ps[:].rearrange("p i (h d) -> p i h d", h=HEADS)
-                    slots = slice(first + 2 * pair, first + 2 * pair + 2)
-                    nc.vector.tensor_tensor(
-                        out=out_slots[:, slots, :, 0:NOPE],
-                        in0=q_heads[:, :, :, 0:NOPE],
-                        in1=bias_pair[:, :, :, 0:NOPE],
-                        op=ADD,
-                    )
-                    nc.vector.tensor_tensor(
-                        out=x_rope[:, 2 * pair : 2 * pair + 2, :, :],
-                        in0=q_heads[:, :, :, NOPE:HEAD_DIM],
-                        in1=bias_pair[:, :, :, NOPE:HEAD_DIM],
-                        op=ADD,
-                    )
+                nc.scalar.copy(
+                    out=grouped_words[:, pair * 2 * P : (pair + 1) * 2 * P, :],
+                    in_=x_t[:].rearrange("p u r -> p r u"),
+                )
+            grouped_of[g] = grouped
 
-                slot0 = c * CHUNK + first
-                in_part = slice(slot0 % TABLE_SLOTS, slot0 % TABLE_SLOTS + GROUP)
-                both_heads = [P, GROUP, HEADS, ROPE]
-                cos_g = cos_parts[slot0 // TABLE_SLOTS][:, in_part, :].unsqueeze(2).to_broadcast(both_heads)
-                sin_g = sin_parts[slot0 // TABLE_SLOTS][:, in_part, :].unsqueeze(2).to_broadcast(both_heads)
-                out_rope = out_slots[:, first : first + GROUP, :, NOPE:HEAD_DIM]
-                turned = stage.tile([P, GROUP, HEADS, ROPE], F32)
-                nc.vector.tensor_tensor(out=out_rope, in0=x_rope[:], in1=cos_g, op=MULT)
-                nc.vector.tensor_tensor(
-                    out=turned[:, :, :, 0:HALF],
-                    in0=x_rope[:, :, :, HALF:ROPE],
-                    in1=sin_g[:, :, :, 0:HALF],
-                    op=MULT,
+        def quantise(g):
+            codes = stage.tile([P, GROUP * P], U32, align_bytes=64)
+            scales = stage.tile([P, GROUP * P], U8, align_bytes=64)
+            nc.vector.quantize_mx(
+                out=codes[:].bitcast(FP8X4), scales=scales[:], in_=grouped_of[g][:]
+            )
+            codes_of[g] = codes
+            scales_of[g] = scales
+
+        def multiply(g):
+            codes = codes_of[g]
+            scales = scales_of[g]
+            q_stay = psum_nope.tile([P, GROUP, P], F32)
+            for i in range(GROUP):
+                cols = slice(i * P, (i + 1) * P)
+                nc.tensor.matmul_mx(
+                    out=q_stay[:, i, :],
+                    lhsT=codes[:, cols].bitcast(FP8X4),
+                    lhsT_scale=scales[:, cols],
+                    rhs=w_codes[:, stay].bitcast(FP8X4),
+                    rhs_scale=w_scales[:, stay],
+                    start=True,
+                    stop=True,
                 )
-                nc.vector.tensor_tensor(
-                    out=turned[:, :, :, HALF:ROPE],
-                    in0=x_rope[:, :, :, 0:HALF],
-                    in1=sin_g[:, :, :, HALF:ROPE],
-                    op=MULT,
+            q_turn_t = psum_rope_t.tile([P, GROUP * P], F32)
+            nc.tensor.matmul_mx(
+                out=q_turn_t[:],
+                lhsT=w_codes[:, turn].bitcast(FP8X4),
+                lhsT_scale=w_scales[:, turn],
+                rhs=codes[:].bitcast(FP8X4),
+                rhs_scale=scales[:],
+                start=True,
+                stop=True,
+            )
+            q_stay_of[g] = q_stay
+            q_turn_t_of[g] = q_turn_t
+
+        def add_turn_bias(g):
+            x_turn_t = stage.tile([P, GROUP * P], F32)
+            nc.scalar.activation(
+                out=x_turn_t[:], in_=q_turn_t_of[g][:], func=IDENTITY, bias=bias_turn[:], scale=1.0
+            )
+            x_turn_t_of[g] = x_turn_t
+
+        def transpose_back(g):
+            x_turn = psum_rope.tile([P, GROUP, P], F32)
+            for i in range(GROUP):
+                nc.tensor.transpose(
+                    x_turn[:, i, :], x_turn_t_of[g][:, i * P : (i + 1) * P], ident[:]
                 )
-                nc.vector.tensor_tensor(
-                    out=out_rope[:, :, :, 0:HALF],
-                    in0=out_rope[:, :, :, 0:HALF],
-                    in1=turned[:, :, :, 0:HALF],
-                    op=SUBTRACT,
+            x_turn_of[g] = x_turn
+
+        def out_slots(g):
+            first = (g % CHUNK_GROUPS) * GROUP
+            by_slot = out_of[g // CHUNK_GROUPS][:].rearrange("p h t d -> p t h d")
+            return by_slot[:, first : first + GROUP]
+
+        def finish_stay(g):
+            if g % CHUNK_GROUPS == 0:
+                out_sb = resident.tile([P, HEADS, CHUNK, HEAD_DIM], F32)
+                out_of[g // CHUNK_GROUPS] = out_sb
+            nc.vector.tensor_tensor(
+                out=out_slots(g)[:, :, :, 0:NOPE],
+                in0=q_stay_of[g][:].rearrange("p i (h d) -> p i h d", h=HEADS),
+                in1=bias_stay[:].unsqueeze(1).to_broadcast([P, GROUP, HEADS, NOPE]),
+                op=ADD,
+            )
+
+        def rotate(g):
+            slot0 = g * GROUP
+            in_part = slice(slot0 % TABLE_SLOTS, slot0 % TABLE_SLOTS + GROUP)
+            both_heads = [P, GROUP, HEADS, ROPE]
+            cos_g = cos_parts[slot0 // TABLE_SLOTS][:, in_part, :].unsqueeze(2).to_broadcast(both_heads)
+            sin_g = sin_parts[slot0 // TABLE_SLOTS][:, in_part, :].unsqueeze(2).to_broadcast(both_heads)
+            x_turn = x_turn_of[g][:].rearrange("p i (h d) -> p i h d", h=HEADS)
+            out_rope = out_slots(g)[:, :, :, NOPE:HEAD_DIM]
+            turned = stage.tile([P, GROUP, HEADS, ROPE], F32)
+            low = slice(0, HALF)
+            high = slice(HALF, ROPE)
+            nc.vector.tensor_tensor(out=out_rope, in0=x_turn, in1=cos_g, op=MULT)
+            nc.vector.tensor_tensor(
+                out=turned[:, :, :, low], in0=x_turn[:, :, :, high], in1=sin_g[:, :, :, low], op=MULT
+            )
+            nc.vector.tensor_tensor(
+                out=turned[:, :, :, high], in0=x_turn[:, :, :, low], in1=sin_g[:, :, :, high], op=MULT
+            )
+            nc.gpsimd.tensor_tensor(
+                out=out_rope[:, :, :, low],
+                in0=out_rope[:, :, :, low],
+                in1=turned[:, :, :, low],
+                op=SUBTRACT,
+            )
+            nc.gpsimd.tensor_tensor(
+                out=out_rope[:, :, :, high],
+                in0=out_rope[:, :, :, high],
+                in1=turned[:, :, :, high],
+                op=ADD,
+            )
+            if g % CHUNK_GROUPS == CHUNK_GROUPS - 1:
+                c = g // CHUNK_GROUPS
+                nc.sync.dma_start(
+                    out=out_view[:, :, c * CHUNK : (c + 1) * CHUNK, :], in_=out_of[c][:]
                 )
-                nc.vector.tensor_tensor(
-                    out=out_rope[:, :, :, HALF:ROPE],
-                    in0=out_rope[:, :, :, HALF:ROPE],
-                    in1=turned[:, :, :, HALF:ROPE],
-                    op=ADD,
-                )
-            nc.sync.dma_start(out=out_view[:, :, c * CHUNK : (c + 1) * CHUNK, :], in_=out_sb[:])
+
+        for s in range(GROUPS + 3):
+            if 0 <= s - 2 < GROUPS:
+                add_turn_bias(s - 2)
+            if s < GROUPS:
+                transpose_hidden(s)
+            if 0 <= s - 2 < GROUPS:
+                transpose_back(s - 2)
+            if 0 <= s - 1 < GROUPS:
+                quantise(s - 1)
+                multiply(s - 1)
+            if 0 <= s - 2 < GROUPS:
+                finish_stay(s - 2)
+            if 0 <= s - 3:
+                rotate(s - 3)

@@ -25,6 +25,7 @@ SLOTS = TOKENS // P
 GROUP = 4
 GROUPS = SLOTS // GROUP
 CHUNK = 8
+CHUNKS = SLOTS // CHUNK
 CHUNK_GROUPS = CHUNK // GROUP
 TABLE_SLOTS = 32
 
@@ -39,7 +40,7 @@ def tile_gptossmlaattention_pb_t_kernel(tc, hidden_states, cos, sin, Wq, bq, out
     out_view = out.flatten_outer_dims().rearrange("(h p t) d -> p h t d", h=HEADS, t=SLOTS)
 
     with tc.tile_pool(name="const", bufs=1) as const, tc.tile_pool(
-        name="resident", bufs=SLOTS // CHUNK
+        name="resident", bufs=CHUNKS
     ) as resident, tc.tile_pool(name="tables", bufs=SLOTS // TABLE_SLOTS) as tables, tc.tile_pool(
         name="stage", bufs=3
     ) as stage, tc.psum_pool(name="psum_setup", bufs=1) as psum_setup, tc.psum_pool(
@@ -47,20 +48,42 @@ def tile_gptossmlaattention_pb_t_kernel(tc, hidden_states, cos, sin, Wq, bq, out
     ) as psum_t, tc.psum_pool(name="psum_nope", bufs=2) as psum_nope, tc.psum_pool(
         name="psum_rope_t", bufs=1
     ) as psum_rope_t, tc.psum_pool(name="psum_rope", bufs=2) as psum_rope, tc.manual_schedule():
-        w_raw = const.tile([P, PACK, FEATURES], BF16)
-        for u in range(2):
+        bias_row = const.tile([P, FEATURES], BF16)
+        nc.vector.memset(bias_row[:], 0.0)
+        bq_by_kind = bq.rearrange("(o h x d) -> o x h d", o=1, h=HEADS, x=2)
+        for x in range(2):
             nc.sync.dma_start(
-                out=w_raw[:, 2 * u : 2 * u + 2, :],
-                in_=Wq[256 * u : 256 * u + 256, :].rearrange("(p e) c -> p e c", e=2),
+                out=bias_row[0:1, x * P : (x + 1) * P].rearrange("o (h d) -> o h d", h=HEADS),
+                in_=bq_by_kind[:, x],
             )
+
         x_chunks = []
+        for c in range(CHUNKS):
+            x_sb = resident.tile([P, CHUNK, HID], BF16)
+            x_chunks.append(x_sb)
+
+        def load_hidden(slot0, count):
+            first = slot0 % CHUNK
+            nc.sync.dma_start(
+                out=x_chunks[slot0 // CHUNK][:, first : first + count, :],
+                in_=hidden_view[:, slot0 : slot0 + count, :],
+            )
+
+        w_raw = const.tile([P, PACK, FEATURES], BF16)
         cos_parts = []
         sin_parts = []
-        for c in range(SLOTS // CHUNK):
-            x_sb = resident.tile([P, CHUNK, HID], BF16)
-            nc.sync.dma_start(out=x_sb[:], in_=hidden_view[:, c * CHUNK : (c + 1) * CHUNK, :])
-            x_chunks.append(x_sb)
-            if c % (TABLE_SLOTS // CHUNK) == 0:
+        for c in range(CHUNKS):
+            if c == 0:
+                load_hidden(0, GROUP)
+                for u in range(2):
+                    nc.sync.dma_start(
+                        out=w_raw[:, 2 * u : 2 * u + 2, :],
+                        in_=Wq[256 * u : 256 * u + 256, :].rearrange("(p e) c -> p e c", e=2),
+                    )
+                load_hidden(GROUP, GROUP)
+            else:
+                load_hidden(c * CHUNK, CHUNK)
+            if (c * CHUNK) % TABLE_SLOTS == 0:
                 part = slice(c * CHUNK, c * CHUNK + TABLE_SLOTS)
                 cos_sb = tables.tile([P, TABLE_SLOTS, ROPE], BF16)
                 nc.sync.dma_start(out=cos_sb[:], in_=cos_view[:, part, :])
@@ -74,16 +97,9 @@ def tile_gptossmlaattention_pb_t_kernel(tc, hidden_states, cos, sin, Wq, bq, out
 
         w_grouped = const.tile([P, 2, P, PACK], BF16, align_bytes=64)
         w_by_kind = w_raw[:].rearrange("p t (h x d) -> p x h d t", h=HEADS, x=2)
-        bq_by_kind = bq.rearrange("(o h x d) -> o x h d", o=1, h=HEADS, x=2)
-        bias_row = const.tile([P, FEATURES], BF16)
-        nc.vector.memset(bias_row[:], 0.0)
         ones = const.tile([P, P], BF16)
         nc.vector.memset(ones[:], 1.0)
         for x in range(2):
-            nc.scalar.dma_start(
-                out=bias_row[0:1, x * P : (x + 1) * P].rearrange("o (h d) -> o h d", h=HEADS),
-                in_=bq_by_kind[:, x],
-            )
             nc.vector.tensor_copy(
                 out=w_grouped[:, x].rearrange("p (h d) t -> p h d t", h=HEADS), in_=w_by_kind[:, x]
             )
@@ -242,8 +258,14 @@ def tile_gptossmlaattention_pb_t_kernel(tc, hidden_states, cos, sin, Wq, bq, out
                 in1=turned[:, :, :, high],
                 op=ADD,
             )
-            if g % CHUNK_GROUPS == CHUNK_GROUPS - 1:
-                c = g // CHUNK_GROUPS
+            c = g // CHUNK_GROUPS
+            first = (g % CHUNK_GROUPS) * GROUP
+            if c == CHUNKS - 1:
+                nc.sync.dma_start(
+                    out=out_view[:, :, slot0 : slot0 + GROUP, :],
+                    in_=out_of[c][:, :, first : first + GROUP, :],
+                )
+            elif first + GROUP == CHUNK:
                 nc.sync.dma_start(
                     out=out_view[:, :, c * CHUNK : (c + 1) * CHUNK, :], in_=out_of[c][:]
                 )

@@ -43,11 +43,7 @@ def tile_gptossmlaattention_pb_t_kernel(tc, hidden_states, cos, sin, Wq, bq, out
         name="resident", bufs=CHUNKS
     ) as resident, tc.tile_pool(name="tables", bufs=SLOTS // TABLE_SLOTS) as tables, tc.tile_pool(
         name="stage", bufs=3
-    ) as stage, tc.psum_pool(name="psum_setup", bufs=1) as psum_setup, tc.psum_pool(
-        name="psum_t", bufs=2
-    ) as psum_t, tc.psum_pool(name="psum_nope", bufs=2) as psum_nope, tc.psum_pool(
-        name="psum_rope_t", bufs=1
-    ) as psum_rope_t, tc.psum_pool(name="psum_rope", bufs=2) as psum_rope, tc.manual_schedule():
+    ) as stage, tc.psum_pool(name="psum", bufs=2) as psum, tc.manual_schedule():
         bias_row = const.tile([P, FEATURES], BF16)
         nc.vector.memset(bias_row[:], 0.0)
         bq_by_kind = bq.rearrange("(o h x d) -> o x h d", o=1, h=HEADS, x=2)
@@ -83,8 +79,8 @@ def tile_gptossmlaattention_pb_t_kernel(tc, hidden_states, cos, sin, Wq, bq, out
                 load_hidden(GROUP, GROUP)
             else:
                 load_hidden(c * CHUNK, CHUNK)
-            if (c * CHUNK) % TABLE_SLOTS == 0:
-                part = slice(c * CHUNK, c * CHUNK + TABLE_SLOTS)
+            if ((c - 1) * CHUNK) % TABLE_SLOTS == 0:
+                part = slice((c - 1) * CHUNK, (c - 1) * CHUNK + TABLE_SLOTS)
                 cos_sb = tables.tile([P, TABLE_SLOTS, ROPE], BF16)
                 nc.sync.dma_start(out=cos_sb[:], in_=cos_view[:, part, :])
                 cos_parts.append(cos_sb)
@@ -113,7 +109,7 @@ def tile_gptossmlaattention_pb_t_kernel(tc, hidden_states, cos, sin, Wq, bq, out
         stay = slice(0, P)
         turn = slice(P, 2 * P)
 
-        setup_ps = psum_setup.tile([P, FEATURES + ROPE], F32)
+        setup_ps = psum.tile([P, FEATURES + ROPE], F32, tag="x_turn")
         nc.tensor.matmul(
             out=setup_ps[:, 0:FEATURES], lhsT=ones[:], rhs=bias_row[:], start=True, stop=True
         )
@@ -146,7 +142,7 @@ def tile_gptossmlaattention_pb_t_kernel(tc, hidden_states, cos, sin, Wq, bq, out
             grouped = stage.tile([P, GROUP * P * PACK], BF16, align_bytes=64)
             grouped_words = grouped[:].bitcast(F32).rearrange("p (r u) -> p r u", u=2)
             for pair in range(GROUP // 2):
-                x_t = psum_t.tile([P, 2, 2 * P], F32)
+                x_t = psum.tile([P, 2, 2 * P], F32)
                 for i in range(2):
                     for u in range(2):
                         nc.tensor.transpose(
@@ -172,7 +168,7 @@ def tile_gptossmlaattention_pb_t_kernel(tc, hidden_states, cos, sin, Wq, bq, out
         def multiply(g):
             codes = codes_of[g]
             scales = scales_of[g]
-            q_stay = psum_nope.tile([P, GROUP, P], F32)
+            q_stay = psum.tile([P, GROUP, P], F32)
             for i in range(GROUP):
                 cols = slice(i * P, (i + 1) * P)
                 nc.tensor.matmul_mx(
@@ -184,7 +180,7 @@ def tile_gptossmlaattention_pb_t_kernel(tc, hidden_states, cos, sin, Wq, bq, out
                     start=True,
                     stop=True,
                 )
-            q_turn_t = psum_rope_t.tile([P, GROUP * P], F32)
+            q_turn_t = psum.tile([P, GROUP * P], F32)
             nc.tensor.matmul_mx(
                 out=q_turn_t[:],
                 lhsT=w_codes[:, turn].bitcast(FP8X4),
@@ -205,7 +201,7 @@ def tile_gptossmlaattention_pb_t_kernel(tc, hidden_states, cos, sin, Wq, bq, out
             x_turn_t_of[g] = x_turn_t
 
         def transpose_back(g):
-            x_turn = psum_rope.tile([P, GROUP, P], F32)
+            x_turn = psum.tile([P, GROUP, P], F32)
             for i in range(GROUP):
                 nc.tensor.transpose(
                     x_turn[:, i, :], x_turn_t_of[g][:, i * P : (i + 1) * P], ident[:]
@@ -270,17 +266,17 @@ def tile_gptossmlaattention_pb_t_kernel(tc, hidden_states, cos, sin, Wq, bq, out
                     out=out_view[:, :, c * CHUNK : (c + 1) * CHUNK, :], in_=out_of[c][:]
                 )
 
-        for s in range(GROUPS + 3):
+        for s in range(GROUPS + 4):
             if 0 <= s - 2 < GROUPS:
                 add_turn_bias(s - 2)
             if s < GROUPS:
                 transpose_hidden(s)
-            if 0 <= s - 2 < GROUPS:
-                transpose_back(s - 2)
+            if 0 <= s - 3 < GROUPS:
+                transpose_back(s - 3)
             if 0 <= s - 1 < GROUPS:
                 quantise(s - 1)
                 multiply(s - 1)
             if 0 <= s - 2 < GROUPS:
                 finish_stay(s - 2)
-            if 0 <= s - 3:
-                rotate(s - 3)
+            if 0 <= s - 4:
+                rotate(s - 4)

import concourse.mybir as mybir
from concourse.masks import make_identity

F32 = mybir.dt.float32
BF16 = mybir.dt.bfloat16
U32 = mybir.dt.uint32
U8 = mybir.dt.uint8
FP8X4 = mybir.dt.float8_e4m3fn_x4
ADD = mybir.AluOpType.add
SUBTRACT = mybir.AluOpType.subtract
MULT = mybir.AluOpType.mult
IDENTITY = mybir.ActivationFunctionType.Identity

P = 128
TOKENS = 8192
HID = 512
HEADS = 2
HEAD_DIM = 128
NOPE = 64
ROPE = 64
HALF = ROPE // 2
FEATURES = HEADS * HEAD_DIM
PACK = 4
SLOTS = TOKENS // P
GROUP = 4
GROUPS = SLOTS // GROUP
CHUNK = 8
CHUNKS = SLOTS // CHUNK
CHUNK_GROUPS = CHUNK // GROUP
TABLE_SLOTS = 32

FLOPS = 2 * TOKENS * HID * FEATURES


def tile_gptossmlaattention_pb_t_kernel(tc, hidden_states, cos, sin, Wq, bq, out):
    nc = tc.nc
    hidden_view = hidden_states.flatten_outer_dims().rearrange("(p t) k -> p t k", t=SLOTS)
    cos_view = cos.flatten_outer_dims().rearrange("(p t) c -> p t c", t=SLOTS)
    sin_view = sin.flatten_outer_dims().rearrange("(p t) c -> p t c", t=SLOTS)
    out_view = out.flatten_outer_dims().rearrange("(h p t) d -> p h t d", h=HEADS, t=SLOTS)

    with tc.tile_pool(name="const", bufs=1) as const, tc.tile_pool(
        name="resident", bufs=CHUNKS
    ) as resident, tc.tile_pool(name="tables", bufs=SLOTS // TABLE_SLOTS) as tables, tc.tile_pool(
        name="stage", bufs=3
    ) as stage, tc.psum_pool(name="psum", bufs=2) as psum, tc.manual_schedule():
        bias_row = const.tile([P, FEATURES], BF16)
        nc.vector.memset(bias_row[:], 0.0)
        bq_by_kind = bq.rearrange("(o h x d) -> o x h d", o=1, h=HEADS, x=2)
        for x in range(2):
            nc.sync.dma_start(
                out=bias_row[0:1, x * P : (x + 1) * P].rearrange("o (h d) -> o h d", h=HEADS),
                in_=bq_by_kind[:, x],
            )

        x_chunks = []
        for c in range(CHUNKS):
            x_sb = resident.tile([P, CHUNK, HID], BF16)
            x_chunks.append(x_sb)

        def load_hidden(slot0, count):
            first = slot0 % CHUNK
            nc.sync.dma_start(
                out=x_chunks[slot0 // CHUNK][:, first : first + count, :],
                in_=hidden_view[:, slot0 : slot0 + count, :],
            )

        w_raw = const.tile([P, PACK, FEATURES], BF16)
        cos_parts = []
        sin_parts = []
        for c in range(CHUNKS):
            if c == 0:
                load_hidden(0, GROUP)
                for u in range(2):
                    nc.sync.dma_start(
                        out=w_raw[:, 2 * u : 2 * u + 2, :],
                        in_=Wq[256 * u : 256 * u + 256, :].rearrange("(p e) c -> p e c", e=2),
                    )
                load_hidden(GROUP, GROUP)
            else:
                load_hidden(c * CHUNK, CHUNK)
            if ((c - 1) * CHUNK) % TABLE_SLOTS == 0:
                part = slice((c - 1) * CHUNK, (c - 1) * CHUNK + TABLE_SLOTS)
                cos_sb = tables.tile([P, TABLE_SLOTS, ROPE], BF16)
                nc.sync.dma_start(out=cos_sb[:], in_=cos_view[:, part, :])
                cos_parts.append(cos_sb)
                sin_sb = tables.tile([P, TABLE_SLOTS, ROPE], BF16)
                nc.sync.dma_start(out=sin_sb[:], in_=sin_view[:, part, :])
                sin_parts.append(sin_sb)

        ident = const.tile([P, P], F32)
        make_identity(nc, ident[:])

        w_grouped = const.tile([P, 2, P, PACK], BF16, align_bytes=64)
        w_by_kind = w_raw[:].rearrange("p t (h x d) -> p x h d t", h=HEADS, x=2)
        ones = const.tile([P, P], BF16)
        nc.vector.memset(ones[:], 1.0)
        for x in range(2):
            nc.vector.tensor_copy(
                out=w_grouped[:, x].rearrange("p (h d) t -> p h d t", h=HEADS), in_=w_by_kind[:, x]
            )
        w_codes = const.tile([P, FEATURES], U32, align_bytes=64)
        w_scales = const.tile([P, FEATURES], U8, align_bytes=64)
        nc.vector.quantize_mx(
            out=w_codes[:].bitcast(FP8X4),
            scales=w_scales[:],
            in_=w_grouped[:].rearrange("p x c t -> p (x c t)"),
        )
        stay = slice(0, P)
        turn = slice(P, 2 * P)

        setup_ps = psum.tile([P, FEATURES + ROPE], F32, tag="x_turn")
        nc.tensor.matmul(
            out=setup_ps[:, 0:FEATURES], lhsT=ones[:], rhs=bias_row[:], start=True, stop=True
        )
        nc.tensor.matmul(
            out=setup_ps[:, FEATURES : FEATURES + ROPE],
            lhsT=bias_row[:, turn],
            rhs=ones[:, 0:ROPE],
            start=True,
            stop=True,
        )
        bias_stay = const.tile([P, HEADS, NOPE], F32)
        nc.vector.tensor_copy(
            out=bias_stay[:], in_=setup_ps[:, stay].rearrange("p (h d) -> p h d", h=HEADS)
        )
        bias_turn = const.tile([P, 1], F32)
        nc.vector.tensor_copy(out=bias_turn[:], in_=setup_ps[:, FEATURES : FEATURES + 1])

        grouped_of = {}
        codes_of = {}
        scales_of = {}
        q_stay_of = {}
        q_turn_t_of = {}
        x_turn_t_of = {}
        x_turn_of = {}
        out_of = {}

        def transpose_hidden(g):
            x_words = x_chunks[g // CHUNK_GROUPS][:].bitcast(F32)
            first = (g % CHUNK_GROUPS) * GROUP
            grouped = stage.tile([P, GROUP * P * PACK], BF16, align_bytes=64)
            grouped_words = grouped[:].bitcast(F32).rearrange("p (r u) -> p r u", u=2)
            for pair in range(GROUP // 2):
                x_t = psum.tile([P, 2, 2 * P], F32)
                for i in range(2):
                    for u in range(2):
                        nc.tensor.transpose(
                            x_t[:, u, i * P : (i + 1) * P],
                            x_words[:, first + 2 * pair + i, u * P : (u + 1) * P],
                            ident[:],
                        )
                nc.scalar.copy(
                    out=grouped_words[:, pair * 2 * P : (pair + 1) * 2 * P, :],
                    in_=x_t[:].rearrange("p u r -> p r u"),
                )
            grouped_of[g] = grouped

        def quantise(g):
            codes = stage.tile([P, GROUP * P], U32, align_bytes=64)
            scales = stage.tile([P, GROUP * P], U8, align_bytes=64)
            nc.vector.quantize_mx(
                out=codes[:].bitcast(FP8X4), scales=scales[:], in_=grouped_of[g][:]
            )
            codes_of[g] = codes
            scales_of[g] = scales

        def multiply(g):
            codes = codes_of[g]
            scales = scales_of[g]
            q_stay = psum.tile([P, GROUP, P], F32)
            for i in range(GROUP):
                cols = slice(i * P, (i + 1) * P)
                nc.tensor.matmul_mx(
                    out=q_stay[:, i, :],
                    lhsT=codes[:, cols].bitcast(FP8X4),
                    lhsT_scale=scales[:, cols],
                    rhs=w_codes[:, stay].bitcast(FP8X4),
                    rhs_scale=w_scales[:, stay],
                    start=True,
                    stop=True,
                )
            q_turn_t = psum.tile([P, GROUP * P], F32)
            nc.tensor.matmul_mx(
                out=q_turn_t[:],
                lhsT=w_codes[:, turn].bitcast(FP8X4),
                lhsT_scale=w_scales[:, turn],
                rhs=codes[:].bitcast(FP8X4),
                rhs_scale=scales[:],
                start=True,
                stop=True,
            )
            q_stay_of[g] = q_stay
            q_turn_t_of[g] = q_turn_t

        def add_turn_bias(g):
            x_turn_t = stage.tile([P, GROUP * P], F32)
            nc.scalar.activation(
                out=x_turn_t[:], in_=q_turn_t_of[g][:], func=IDENTITY, bias=bias_turn[:], scale=1.0
            )
            x_turn_t_of[g] = x_turn_t

        def transpose_back(g):
            x_turn = psum.tile([P, GROUP, P], F32)
            for i in range(GROUP):
                nc.tensor.transpose(
                    x_turn[:, i, :], x_turn_t_of[g][:, i * P : (i + 1) * P], ident[:]
                )
            x_turn_of[g] = x_turn

        def out_slots(g):
            first = (g % CHUNK_GROUPS) * GROUP
            by_slot = out_of[g // CHUNK_GROUPS][:].rearrange("p h t d -> p t h d")
            return by_slot[:, first : first + GROUP]

        def finish_stay(g):
            if g % CHUNK_GROUPS == 0:
                out_sb = resident.tile([P, HEADS, CHUNK, HEAD_DIM], F32)
                out_of[g // CHUNK_GROUPS] = out_sb
            nc.vector.tensor_tensor(
                out=out_slots(g)[:, :, :, 0:NOPE],
                in0=q_stay_of[g][:].rearrange("p i (h d) -> p i h d", h=HEADS),
                in1=bias_stay[:].unsqueeze(1).to_broadcast([P, GROUP, HEADS, NOPE]),
                op=ADD,
            )

        def rotate(g):
            slot0 = g * GROUP
            in_part = slice(slot0 % TABLE_SLOTS, slot0 % TABLE_SLOTS + GROUP)
            both_heads = [P, GROUP, HEADS, ROPE]
            cos_g = cos_parts[slot0 // TABLE_SLOTS][:, in_part, :].unsqueeze(2).to_broadcast(both_heads)
            sin_g = sin_parts[slot0 // TABLE_SLOTS][:, in_part, :].unsqueeze(2).to_broadcast(both_heads)
            x_turn = x_turn_of[g][:].rearrange("p i (h d) -> p i h d", h=HEADS)
            out_rope = out_slots(g)[:, :, :, NOPE:HEAD_DIM]
            turned = stage.tile([P, GROUP, HEADS, ROPE], F32)
            low = slice(0, HALF)
            high = slice(HALF, ROPE)
            nc.vector.tensor_tensor(out=out_rope, in0=x_turn, in1=cos_g, op=MULT)
            nc.vector.tensor_tensor(
                out=turned[:, :, :, low], in0=x_turn[:, :, :, high], in1=sin_g[:, :, :, low], op=MULT
            )
            nc.vector.tensor_tensor(
                out=turned[:, :, :, high], in0=x_turn[:, :, :, low], in1=sin_g[:, :, :, high], op=MULT
            )
            nc.gpsimd.tensor_tensor(
                out=out_rope[:, :, :, low],
                in0=out_rope[:, :, :, low],
                in1=turned[:, :, :, low],
                op=SUBTRACT,
            )
            nc.gpsimd.tensor_tensor(
                out=out_rope[:, :, :, high],
                in0=out_rope[:, :, :, high],
                in1=turned[:, :, :, high],
                op=ADD,
            )
            c = g // CHUNK_GROUPS
            first = (g % CHUNK_GROUPS) * GROUP
            if c == CHUNKS - 1:
                nc.sync.dma_start(
                    out=out_view[:, :, slot0 : slot0 + GROUP, :],
                    in_=out_of[c][:, :, first : first + GROUP, :],
                )
            elif first + GROUP == CHUNK:
                nc.sync.dma_start(
                    out=out_view[:, :, c * CHUNK : (c + 1) * CHUNK, :], in_=out_of[c][:]
                )

        for s in range(GROUPS + 4):
            if 0 <= s - 2 < GROUPS:
                add_turn_bias(s - 2)
            if s < GROUPS:
                transpose_hidden(s)
            if 0 <= s - 3 < GROUPS:
                transpose_back(s - 3)
            if 0 <= s - 1 < GROUPS:
                quantise(s - 1)
                multiply(s - 1)
            if 0 <= s - 2 < GROUPS:
                finish_stay(s - 2)
            if 0 <= s - 4:
                rotate(s - 4)
